import numpy as np
import ml_dtypes


def mxq(x, axis, fmt="e4m3"):
    dtype, down = {"e4m3": (ml_dtypes.float8_e4m3fn, 7), "e5m2": (ml_dtypes.float8_e5m2, 14)}[fmt]
    v = np.moveaxis(np.asarray(x, np.float32).astype(ml_dtypes.bfloat16).astype(np.float64), axis, -1)
    blocks = v.reshape(v.shape[:-1] + (-1, 32))
    amax = np.abs(blocks).max(-1, keepdims=True)
    byte = np.maximum(np.where(amax > 0, np.frexp(amax)[1] - 1 + 127, 0) - down, 1)
    scale = np.exp2(byte - 127.0)
    codes = (blocks / scale).astype(np.float32).astype(dtype).astype(np.float64)
    return np.moveaxis((codes * scale).reshape(v.shape), -1, axis)


WIDE = False


def mx_kscale(k):
    if not WIDE:
        return np.ones(k)
    levels = np.array([10, -10, 5, -5, 0])
    if k % 512:
        return np.exp2(np.random.permutation(np.resize(levels, k // 32))).repeat(32)
    a = np.empty((k // 512, 16))
    for p in range(k // 512):
        a[p, :8] = np.random.permutation(np.resize(levels, 8))
        for g in range(8):
            far = levels[np.abs(levels - a[p, g]) >= 10]
            a[p, g + 8] = far[np.random.randint(len(far))]
    return np.exp2(a.ravel()).repeat(32)


BF16 = ml_dtypes.bfloat16


def bf(x):
    return np.asarray(x, np.float32).astype(BF16)


def f64(x):
    return np.asarray(x).astype(np.float64)


B, S, D, E, WINDOW = 2, 512, 1024, 1024, 10
HALF = WINDOW // 2
NW = HALF + HALF + 1


def setup_inputs():
    s, t = mx_kscale(D), mx_kscale(E)
    pos = np.arange(S)[:, None] + np.arange(NW)[None, :] - HALF
    e = np.exp(np.random.standard_normal((B, S, NW))) * ((pos >= 0) & (pos < S))
    return {"x": bf(np.random.standard_normal((B, S, D)) * s),
            "Wv": bf(np.random.standard_normal((E, D)) / np.sqrt(D) / s[None, :] * t[:, None]),
            "bv": bf(np.random.standard_normal(E) * 0.1 * t),
            "attn_band": bf(e / e.sum(-1, keepdims=True)),
            "Wo": bf(np.random.standard_normal((D, E)) / np.sqrt(E) / t[None, :]),
            "bo": bf(np.random.standard_normal(D) * 0.1)}


def reference(x, Wv, bv, attn_band, Wo, bo):
    v = (mxq(f64(x), 2, "e4m3") @ mxq(f64(Wv), 1, "e4m3").T) + f64(bv)
    a = f64(attn_band)
    ctx = np.zeros((B, S, E))
    for o in range(NW):
        sh = o - HALF
        lo, hi = max(0, -sh), min(S, S - sh)
        ctx[:, lo:hi] += a[:, lo:hi, o:o + 1] * v[:, lo + sh:hi + sh]
    return (mxq(ctx, 2, "e4m3") @ mxq(f64(Wo), 1, "e4m3").T) + f64(bo)

@@ -1,0 +1,328 @@
+from contextlib import ExitStack
+
+import concourse.mybir as mybir
+from concourse.masks import make_identity
+
+F32 = mybir.dt.float32
+BF16 = mybir.dt.bfloat16
+U32 = mybir.dt.uint32
+U8 = mybir.dt.uint8
+FP8X4 = mybir.dt.float8_e4m3fn_x4
+ADD = mybir.AluOpType.add
+
+P = 128
+PACK = 4
+BATCH, SEQ, FEATURES = 2, 512, 1024
+TOKENS = BATCH * SEQ
+TAPS, HALF = 11, 5
+TAP_SLOT = 16
+PASSES = FEATURES // (P * PACK)
+N_TILE = 512
+HALVES = FEATURES // N_TILE
+ROW_PAIRS = FEATURES // (2 * P)
+PAIRS_PER_HALF = ROW_PAIRS // HALVES
+
+WIN_STEP = 112
+MARGIN = (P - WIN_STEP) // 2
+N_WINDOWS = (TOKENS - P) // WIN_STEP + 1
+assert MARGIN >= HALF and (N_WINDOWS - 1) * WIN_STEP + P == TOKENS
+SEAM_WINDOW, SEAM = divmod(SEQ, WIN_STEP)
+assert (SEAM_WINDOW - 1) * WIN_STEP + P <= SEQ and SEAM == P // 2
+
+ROW_PITCH = 136
+
+ROUND = 2
+
+FLOPS = 2 * 2 * TOKENS * FEATURES * FEATURES + 2 * TOKENS * TAPS * FEATURES
+
+
+def window_place(w):
+    lo = 0 if w == 0 else MARGIN
+    hi = P if w == N_WINDOWS - 1 else P - MARGIN
+    return w * WIN_STEP, lo, hi
+
+
+def tile_localattention_pb_kernel(tc, x, Wv, bv, attn_band, Wo, bo, out):
+    nc = tc.nc
+    x_hbm = x.rearrange("b s d -> (b s) d")
+    taps_hbm = attn_band.rearrange("b s o -> (b s) o")
+    out_hbm = out.rearrange("b s d -> (b s) d")
+    out_flat = out.rearrange("b s d -> (b s d)")
+    parked = out_flat[TOKENS * FEATURES - N_WINDOWS * P * ROW_PITCH : TOKENS * FEATURES]
+
+    with ExitStack() as stack:
+        keep = stack.enter_context(tc.tile_pool(name="keep", bufs=1))
+        x_pool = stack.enter_context(tc.tile_pool(name="x_pool", bufs=N_WINDOWS))
+        pairs_pool = stack.enter_context(tc.tile_pool(name="pairs_pool", bufs=3))
+        v_pool = stack.enter_context(tc.tile_pool(name="v_pool", bufs=N_WINDOWS))
+        ctx_pool = stack.enter_context(tc.tile_pool(name="ctx_pool", bufs=3))
+        out_pool = stack.enter_context(tc.tile_pool(name="out_pool", bufs=4))
+        psum = stack.enter_context(tc.psum_pool(name="psum", bufs=4))
+        stack.enter_context(tc.manual_schedule())
+
+        ident = keep.tile([P, P], F32)
+        make_identity(nc, ident[:])
+        ident_bf = keep.tile([P, P], BF16)
+        make_identity(nc, ident_bf[:])
+
+        ones = keep.tile([P, P], BF16)
+        nc.vector.memset(ones[:], 1.0)
+        bias_rows = {}
+        for label, bias in (("bv", bv), ("bo", bo)):
+            bias_row = keep.tile([P, FEATURES], BF16, name=label + "_row")
+            nc.vector.memset(bias_row[:], 0.0)
+            nc.scalar.dma_start(out=bias_row[0:1, :], in_=bias.rearrange("(o n) -> o n", o=1))
+            bias_rows[label] = bias_row
+
+        taps_win = keep.tile([P, N_WINDOWS, TAP_SLOT], BF16)
+        nc.scalar.dma_start(
+            out=taps_win[0:WIN_STEP, :, 0:TAPS],
+            in_=taps_hbm[0 : N_WINDOWS * WIN_STEP, :].rearrange("(w r) o -> r w o", r=WIN_STEP),
+        )
+        nc.scalar.dma_start(
+            out=taps_win[WIN_STEP:P, :, 0:TAPS],
+            in_=taps_hbm[P - WIN_STEP : TOKENS, :].rearrange("(w r) o -> r w o", r=WIN_STEP)[
+                2 * WIN_STEP - P : WIN_STEP
+            ],
+        )
+
+        padded = keep.tile([P, N_WINDOWS, ROW_PITCH], F32)
+        nc.vector.memset(padded[:], 0.0)
+        nc.vector.tensor_copy(out=padded[:, :, 0:TAPS], in_=taps_win[:, :, 0:TAPS])
+        nc.gpsimd.dma_start(
+            out=parked.rearrange("(w p q) -> p w q", p=P, q=ROW_PITCH), in_=padded[:]
+        )
+
+        x_rows = {}
+
+        def load_x(w):
+            first, lo, hi = window_place(w)
+            x_win = x_pool.tile([P, FEATURES], BF16)
+            nc.sync.dma_start(out=x_win[:], in_=x_hbm[first : first + P, :])
+            x_rows[w] = x_win
+
+        load_x(0)
+        wv_rows = keep.tile([P, ROW_PAIRS, 2, FEATURES], BF16)
+        for q in range(ROW_PAIRS):
+            group, upper = divmod(q, 2)
+            nc.sync.dma_start(
+                out=wv_rows[:, q, :, :],
+                in_=Wv[PACK * P * group : PACK * P * (group + 1), :].rearrange(
+                    "(m t) k -> m t k", t=PACK
+                )[:, 2 * upper : 2 * upper + 2, :],
+            )
+        for w in range(1, N_WINDOWS):
+            load_x(w)
+
+        band = keep.tile([P, N_WINDOWS, P], F32)
+        nc.sync.dma_start(
+            out=band[:],
+            in_=parked.rearrange("(w r) -> w r", r=P * ROW_PITCH)[
+                :, HALF : HALF + P * (ROW_PITCH - 1)
+            ].rearrange("w (p q) -> p w q", q=ROW_PITCH - 1)[:, :, 0:P],
+        )
+        nc.gpsimd.memset(band[0:SEAM, SEAM_WINDOW, SEAM:P], 0.0)
+        nc.gpsimd.memset(band[SEAM:P, SEAM_WINDOW, 0:SEAM], 0.0)
+
+        wo_rows = keep.tile([P, ROW_PAIRS, 2, FEATURES], BF16)
+        for q in range(ROW_PAIRS):
+            nc.sync.dma_start(
+                out=wo_rows[:, q, :, :],
+                in_=Wo[2 * P * q : 2 * P * (q + 1), :].rearrange("(j m) k -> m j k", m=P),
+            )
+
+        band_t = keep.tile([P, N_WINDOWS, P], F32)
+
+        def transpose_band():
+            for w0 in range(0, N_WINDOWS, PACK):
+                count = min(PACK, N_WINDOWS - w0)
+                flipped = psum.tile([P, PACK, P], F32, tag="flipped")
+                for j in range(count):
+                    nc.tensor.transpose(flipped[:, j, :], band[:, w0 + j, :], ident[:])
+                nc.scalar.copy(out=band_t[:, w0 : w0 + count, :], in_=flipped[:, 0:count, :])
+
+        def transpose_rows(rows, pairs, copy):
+            words = rows.bitcast(F32)
+            flipped = psum.tile([P, PACK, P], F32, tag="flipped")
+            for c in range(PASSES):
+                for u in range(2):
+                    nc.tensor.transpose(
+                        flipped[:, 2 * c + u, :],
+                        words[:, 2 * P * c + u : 2 * P * (c + 1) : 2],
+                        ident[:],
+                    )
+            copy(out=pairs, in_=flipped[:].rearrange("p (c u) r -> p c r u", u=2))
+
+        x_codes = keep.tile([P, N_WINDOWS, PASSES, P], U32, align_bytes=64)
+        x_scales = keep.tile([P, N_WINDOWS, PASSES, P], U8, align_bytes=64)
+
+        def prepare_x(w):
+            x_pairs = pairs_pool.tile([P, PASSES, P, 2], F32, align_bytes=64)
+            transpose_rows(x_rows[w][:], x_pairs[:], nc.scalar.copy)
+            nc.vector.quantize_mx(
+                out=x_codes[:, w, :, :].rearrange("p c r -> p (c r)").bitcast(FP8X4),
+                scales=x_scales[:, w, :, :].rearrange("p c r -> p (c r)"),
+                in_=x_pairs[:].rearrange("p c r u -> p (c r u)").bitcast(BF16),
+            )
+
+        def weight_tiles(label):
+            codes = keep.tile([P, PASSES, FEATURES], U32, name=label + "_codes", align_bytes=64)
+            scales = keep.tile([P, PASSES, FEATURES], U8, name=label + "_scales", align_bytes=64)
+            return codes, scales
+
+        def prepare_weight_pair(rows, tiles, q):
+            codes, scales = tiles
+            w_pairs = pairs_pool.tile([P, PASSES, 2 * P, 2], F32, align_bytes=64)
+            transpose_rows(rows[:, q, 0, :], w_pairs[:, :, 0:P, :], nc.scalar.copy)
+            transpose_rows(rows[:, q, 1, :], w_pairs[:, :, P : 2 * P, :], nc.vector.tensor_copy)
+            cols = slice(2 * P * q, 2 * P * (q + 1))
+            for c in range(PASSES):
+                nc.vector.quantize_mx(
+                    out=codes[:, c, cols].bitcast(FP8X4),
+                    scales=scales[:, c, cols],
+                    in_=w_pairs[:, c, :, :].rearrange("p n u -> p (n u)").bitcast(BF16),
+                )
+
+        wv_tiles = weight_tiles("wv")
+        wo_tiles = weight_tiles("wo")
+
+        def product(acc, left_codes, left_scales, tiles, half):
+            codes, scales = tiles
+            cols = slice(half * N_TILE, (half + 1) * N_TILE)
+            for c in range(PASSES):
+                nc.tensor.matmul_mx(
+                    out=acc,
+                    lhsT=left_codes[c].bitcast(FP8X4),
+                    lhsT_scale=left_scales[c],
+                    rhs=codes[:, c, cols].bitcast(FP8X4),
+                    rhs_scale=scales[:, c, cols],
+                    start=(c == 0),
+                    stop=(c == PASSES - 1),
+                )
+
+        bv_all = keep.tile([P, FEATURES], F32)
+        bo_all = keep.tile([P, FEATURES], F32)
+
+        def spread_biases():
+            for half in range(HALVES):
+                cols = slice(half * N_TILE, (half + 1) * N_TILE)
+                bv_acc = psum.tile([P, N_TILE], F32, tag="acc")
+                nc.tensor.matmul(
+                    out=bv_acc[:], lhsT=ones[:], rhs=bias_rows["bv"][:, cols], start=True, stop=True
+                )
+                nc.scalar.copy(
+                    out=bv_all[:, cols].rearrange("p (t m) -> p t m", t=PACK),
+                    in_=bv_acc[:].rearrange("p (m t) -> p t m", t=PACK),
+                )
+                bo_acc = psum.tile([P, N_TILE], F32, tag="acc")
+                nc.tensor.matmul(
+                    out=bo_acc[:], lhsT=ones[:], rhs=bias_rows["bo"][:, cols], start=True, stop=True
+                )
+                nc.scalar.copy(out=bo_all[:, cols], in_=bo_acc[:])
+
+        v_rows = {}
+
+        def project_v(w):
+            v_win = v_pool.tile([P, FEATURES], F32)
+            for half in range(HALVES):
+                cols = slice(half * N_TILE, (half + 1) * N_TILE)
+                v_acc = psum.tile([P, N_TILE], F32, tag="acc")
+                product(
+                    v_acc[:],
+                    [x_codes[:, w, c, :] for c in range(PASSES)],
+                    [x_scales[:, w, c, :] for c in range(PASSES)],
+                    wv_tiles,
+                    half,
+                )
+                nc.vector.tensor_tensor(
+                    out=v_win[:, cols], in0=v_acc[:], in1=bv_all[:, cols], op=ADD
+                )
+            v_rows[w] = v_win
+
+        ctx_rows = {}
+
+        def mix(w):
+            ctx_win = ctx_pool.tile([P, FEATURES], BF16)
+            for half in range(HALVES):
+                cols = slice(half * N_TILE, (half + 1) * N_TILE)
+                mix_acc = psum.tile([P, N_TILE], F32, tag="acc")
+                nc.tensor.matmul(
+                    out=mix_acc[:],
+                    lhsT=band_t[:, w, :],
+                    rhs=v_rows[w][:, cols],
+                    start=True,
+                    stop=True,
+                )
+                nc.scalar.copy(out=ctx_win[:, cols], in_=mix_acc[:])
+            ctx_rows[w] = ctx_win
+
+        ctx_quads = keep.tile([P, PASSES, TOKENS, PACK], BF16, align_bytes=64)
+        ctx_codes = keep.tile([P, PASSES, TOKENS], U32, align_bytes=64)
+        ctx_scales = keep.tile([P, PASSES, TOKENS], U8, align_bytes=64)
+
+        def flip_ctx(w):
+            first, lo, hi = window_place(w)
+            for c in range(PASSES):
+                flipped = psum.tile([P, PACK, P], BF16, tag="flipped")
+                for t in range(PACK):
+                    blk = c * PACK + t
+                    nc.tensor.transpose(
+                        flipped[:, t, :], ctx_rows[w][:, blk * P : (blk + 1) * P], ident_bf[:]
+                    )
+                copy = nc.scalar.copy if c == 0 else nc.vector.tensor_copy
+                copy(
+                    out=ctx_quads[:, c, first + lo : first + hi, :],
+                    in_=flipped[:, :, lo:hi].rearrange("p t i -> p i t"),
+                )
+
+        def quantise_ctx(tb):
+            tokens = slice(tb * P, (tb + 1) * P)
+            for c in range(PASSES):
+                nc.vector.quantize_mx(
+                    out=ctx_codes[:, c, tokens].bitcast(FP8X4),
+                    scales=ctx_scales[:, c, tokens],
+                    in_=ctx_quads[:, c, tokens, :].rearrange("p i t -> p (i t)"),
+                )
+
+        def project_out(tb):
+            tokens = slice(tb * P, (tb + 1) * P)
+            for half in range(HALVES):
+                cols = slice(half * N_TILE, (half + 1) * N_TILE)
+                out_acc = psum.tile([P, N_TILE], F32, tag="acc")
+                product(
+                    out_acc[:],
+                    [ctx_codes[:, c, tokens] for c in range(PASSES)],
+                    [ctx_scales[:, c, tokens] for c in range(PASSES)],
+                    wo_tiles,
+                    half,
+                )
+                out_sb = out_pool.tile([P, N_TILE], F32)
+                nc.vector.tensor_tensor(out=out_sb[:], in0=out_acc[:], in1=bo_all[:, cols], op=ADD)
+                nc.sync.dma_start(out=out_hbm[tokens, cols], in_=out_sb[:])
+
+        prepare_x(0)
+        spread_biases()
+        for q in range(ROW_PAIRS):
+            prepare_weight_pair(wv_rows, wv_tiles, q)
+        for w in range(1, ROUND):
+            prepare_x(w)
+        for first_w in range(0, N_WINDOWS, ROUND):
+            for w in range(first_w + ROUND, min(first_w + 2 * ROUND, N_WINDOWS)):
+                prepare_x(w)
+            if first_w + ROUND >= N_WINDOWS:
+                transpose_band()
+            for w in range(first_w, min(first_w + ROUND, N_WINDOWS)):
+                project_v(w)
+
+        for w in range(N_WINDOWS + 1):
+            if w < N_WINDOWS:
+                mix(w)
+            if w >= 2:
+                project_out(w - 2)
+            if w < HALVES:
+                for q in range(w * PAIRS_PER_HALF, (w + 1) * PAIRS_PER_HALF):
+                    prepare_weight_pair(wo_rows, wo_tiles, q)
+            if w < N_WINDOWS:
+                flip_ctx(w)
+            if 1 <= w < N_WINDOWS:
+                quantise_ctx(w - 1)

@@ -55,15 +55,12 @@ def tile_localattention_pb_kernel(tc, x, Wv, bv, attn_band, Wo, bo, out):
         x_pool = stack.enter_context(tc.tile_pool(name="x_pool", bufs=N_WINDOWS))
         pairs_pool = stack.enter_context(tc.tile_pool(name="pairs_pool", bufs=3))
         v_pool = stack.enter_context(tc.tile_pool(name="v_pool", bufs=N_WINDOWS))
-        ctx_pool = stack.enter_context(tc.tile_pool(name="ctx_pool", bufs=3))
         out_pool = stack.enter_context(tc.tile_pool(name="out_pool", bufs=4))
         psum = stack.enter_context(tc.psum_pool(name="psum", bufs=4))
         stack.enter_context(tc.manual_schedule())
 
         ident = keep.tile([P, P], F32)
         make_identity(nc, ident[:])
-        ident_bf = keep.tile([P, P], BF16)
-        make_identity(nc, ident_bf[:])
 
         ones = keep.tile([P, P], BF16)
         nc.vector.memset(ones[:], 1.0)
@@ -239,40 +236,27 @@ def tile_localattention_pb_kernel(tc, x, Wv, bv, attn_band, Wo, bo, out):
                 )
             v_rows[w] = v_win
 
-        ctx_rows = {}
-
-        def mix(w):
-            ctx_win = ctx_pool.tile([P, FEATURES], BF16)
-            for half in range(HALVES):
-                cols = slice(half * N_TILE, (half + 1) * N_TILE)
-                mix_acc = psum.tile([P, N_TILE], F32, tag="acc")
-                nc.tensor.matmul(
-                    out=mix_acc[:],
-                    lhsT=band_t[:, w, :],
-                    rhs=v_rows[w][:, cols],
-                    start=True,
-                    stop=True,
-                )
-                nc.scalar.copy(out=ctx_win[:, cols], in_=mix_acc[:])
-            ctx_rows[w] = ctx_win
-
         ctx_quads = keep.tile([P, PASSES, TOKENS, PACK], BF16, align_bytes=64)
         ctx_codes = keep.tile([P, PASSES, TOKENS], U32, align_bytes=64)
         ctx_scales = keep.tile([P, PASSES, TOKENS], U8, align_bytes=64)
 
-        def flip_ctx(w):
+        def mix(w):
             first, lo, hi = window_place(w)
             for c in range(PASSES):
-                flipped = psum.tile([P, PACK, P], BF16, tag="flipped")
+                mixed = psum.tile([P, PACK, P], F32, tag="flipped")
                 for t in range(PACK):
                     blk = c * PACK + t
-                    nc.tensor.transpose(
-                        flipped[:, t, :], ctx_rows[w][:, blk * P : (blk + 1) * P], ident_bf[:]
+                    nc.tensor.matmul(
+                        out=mixed[:, t, lo:hi],
+                        lhsT=v_rows[w][:, blk * P : (blk + 1) * P],
+                        rhs=band_t[:, w, lo:hi],
+                        start=True,
+                        stop=True,
                     )
                 copy = nc.scalar.copy if c == 0 else nc.vector.tensor_copy
                 copy(
                     out=ctx_quads[:, c, first + lo : first + hi, :],
-                    in_=flipped[:, :, lo:hi].rearrange("p t i -> p i t"),
+                    in_=mixed[:, :, lo:hi].rearrange("p t i -> p i t"),
                 )
 
         def quantise_ctx(tb):
@@ -322,7 +306,5 @@ def tile_localattention_pb_kernel(tc, x, Wv, bv, attn_band, Wo, bo, out):
             if w < HALVES:
                 for q in range(w * PAIRS_PER_HALF, (w + 1) * PAIRS_PER_HALF):
                     prepare_weight_pair(wo_rows, wo_tiles, q)
-            if w < N_WINDOWS:
-                flip_ctx(w)
             if 1 <= w < N_WINDOWS:
                 quantise_ctx(w - 1)

@@ -62,12 +62,17 @@ def tile_localattention_pb_kernel(tc, x, Wv, bv, attn_band, Wo, bo, out):
         ident = keep.tile([P, P], F32)
         make_identity(nc, ident[:])
 
+        table_in = keep.tile([P, 1], F32)
+        nc.vector.memset(table_in[:], 0.0)
+        table_out = keep.tile([P, 1], F32)
+        nc.scalar.copy(out=table_out[:], in_=table_in[:])
+
         ones = keep.tile([P, P], BF16)
         nc.vector.memset(ones[:], 1.0)
         bias_rows = {}
         for label, bias in (("bv", bv), ("bo", bo)):
             bias_row = keep.tile([P, FEATURES], BF16, name=label + "_row")
-            nc.vector.memset(bias_row[:], 0.0)
+            nc.vector.memset(bias_row[:].bitcast(mybir.dt.int32), 0)
             nc.scalar.dma_start(out=bias_row[0:1, :], in_=bias.rearrange("(o n) -> o n", o=1))
             bias_rows[label] = bias_row
 
@@ -84,8 +89,8 @@ def tile_localattention_pb_kernel(tc, x, Wv, bv, attn_band, Wo, bo, out):
         )
 
         padded = keep.tile([P, N_WINDOWS, ROW_PITCH], F32)
-        nc.vector.memset(padded[:], 0.0)
-        nc.vector.tensor_copy(out=padded[:, :, 0:TAPS], in_=taps_win[:, :, 0:TAPS])
+        nc.gpsimd.memset(padded[:], 0.0)
+        nc.gpsimd.tensor_copy(out=padded[:, :, 0:TAPS], in_=taps_win[:, :, 0:TAPS])
         nc.gpsimd.dma_start(
             out=parked.rearrange("(w p q) -> p w q", p=P, q=ROW_PITCH), in_=padded[:]
         )
@@ -285,9 +290,9 @@ def tile_localattention_pb_kernel(tc, x, Wv, bv, attn_band, Wo, bo, out):
                 nc.sync.dma_start(out=out_hbm[tokens, cols], in_=out_sb[:])
 
         prepare_x(0)
-        spread_biases()
         for q in range(ROW_PAIRS):
             prepare_weight_pair(wv_rows, wv_tiles, q)
+        spread_biases()
         for w in range(1, ROUND):
             prepare_x(w)
         for first_w in range(0, N_WINDOWS, ROUND):

@@ -20,7 +20,6 @@ PASSES = FEATURES // (P * PACK)
 N_TILE = 512
 HALVES = FEATURES // N_TILE
 ROW_PAIRS = FEATURES // (2 * P)
-PAIRS_PER_HALF = ROW_PAIRS // HALVES
 
 WIN_STEP = 112
 MARGIN = (P - WIN_STEP) // 2
@@ -53,6 +52,7 @@ def tile_localattention_pb_kernel(tc, x, Wv, bv, attn_band, Wo, bo, out):
     with ExitStack() as stack:
         keep = stack.enter_context(tc.tile_pool(name="keep", bufs=1))
         x_pool = stack.enter_context(tc.tile_pool(name="x_pool", bufs=N_WINDOWS))
+        sorted_pool = stack.enter_context(tc.tile_pool(name="sorted_pool", bufs=2))
         pairs_pool = stack.enter_context(tc.tile_pool(name="pairs_pool", bufs=3))
         v_pool = stack.enter_context(tc.tile_pool(name="v_pool", bufs=N_WINDOWS))
         out_pool = stack.enter_context(tc.tile_pool(name="out_pool", bufs=4))
@@ -116,6 +116,13 @@ def tile_localattention_pb_kernel(tc, x, Wv, bv, attn_band, Wo, bo, out):
         for w in range(1, N_WINDOWS):
             load_x(w)
 
+        wo_rows = keep.tile([P, ROW_PAIRS, 2, FEATURES], BF16)
+        for q in range(ROW_PAIRS):
+            nc.sync.dma_start(
+                out=wo_rows[:, q, :, :],
+                in_=Wo[2 * P * q : 2 * P * (q + 1), :].rearrange("(j m) k -> m j k", m=P),
+            )
+
         band = keep.tile([P, N_WINDOWS, P], F32)
         nc.sync.dma_start(
             out=band[:],
@@ -125,13 +132,6 @@ def tile_localattention_pb_kernel(tc, x, Wv, bv, attn_band, Wo, bo, out):
         )
         nc.gpsimd.memset(band[0:SEAM, SEAM_WINDOW, SEAM:P], 0.0)
         nc.gpsimd.memset(band[SEAM:P, SEAM_WINDOW, 0:SEAM], 0.0)
-
-        wo_rows = keep.tile([P, ROW_PAIRS, 2, FEATURES], BF16)
-        for q in range(ROW_PAIRS):
-            nc.sync.dma_start(
-                out=wo_rows[:, q, :, :],
-                in_=Wo[2 * P * q : 2 * P * (q + 1), :].rearrange("(j m) k -> m j k", m=P),
-            )
 
         band_t = keep.tile([P, N_WINDOWS, P], F32)
 
@@ -143,16 +143,18 @@ def tile_localattention_pb_kernel(tc, x, Wv, bv, attn_band, Wo, bo, out):
                     nc.tensor.transpose(flipped[:, j, :], band[:, w0 + j, :], ident[:])
                 nc.scalar.copy(out=band_t[:, w0 : w0 + count, :], in_=flipped[:, 0:count, :])
 
-        def transpose_rows(rows, pairs, copy):
-            words = rows.bitcast(F32)
+        def sort_words(words, count, copy):
+            sorted_words = sorted_pool.tile([P, count, PACK, P], F32, tag="sorted" + str(count))
+            copy(
+                out=sorted_words[:].rearrange("p n (c u) i -> p (n c) u i", u=2),
+                in_=words.rearrange("p (n i u) -> p n u i", i=P, u=2),
+            )
+            return sorted_words
+
+        def transpose_rows(words, pairs, copy):
             flipped = psum.tile([P, PACK, P], F32, tag="flipped")
-            for c in range(PASSES):
-                for u in range(2):
-                    nc.tensor.transpose(
-                        flipped[:, 2 * c + u, :],
-                        words[:, 2 * P * c + u : 2 * P * (c + 1) : 2],
-                        ident[:],
-                    )
+            for j in range(PACK):
+                nc.tensor.transpose(flipped[:, j, :], words[:, j, :], ident[:])
             copy(out=pairs, in_=flipped[:].rearrange("p (c u) r -> p c r u", u=2))
 
         x_codes = keep.tile([P, N_WINDOWS, PASSES, P], U32, align_bytes=64)
@@ -160,7 +162,8 @@ def tile_localattention_pb_kernel(tc, x, Wv, bv, attn_band, Wo, bo, out):
 
         def prepare_x(w):
             x_pairs = pairs_pool.tile([P, PASSES, P, 2], F32, align_bytes=64)
-            transpose_rows(x_rows[w][:], x_pairs[:], nc.scalar.copy)
+            x_sorted = sort_words(x_rows[w][:].bitcast(F32), 1, nc.scalar.copy)
+            transpose_rows(x_sorted[:, 0, :, :], x_pairs[:], nc.scalar.copy)
             nc.vector.quantize_mx(
                 out=x_codes[:, w, :, :].rearrange("p c r -> p (c r)").bitcast(FP8X4),
                 scales=x_scales[:, w, :, :].rearrange("p c r -> p (c r)"),
@@ -172,11 +175,11 @@ def tile_localattention_pb_kernel(tc, x, Wv, bv, attn_band, Wo, bo, out):
             scales = keep.tile([P, PASSES, FEATURES], U8, name=label + "_scales", align_bytes=64)
             return codes, scales
 
-        def prepare_weight_pair(rows, tiles, q):
+        def prepare_weight_pair(w_sorted, tiles, q, second_copy):
             codes, scales = tiles
             w_pairs = pairs_pool.tile([P, PASSES, 2 * P, 2], F32, align_bytes=64)
-            transpose_rows(rows[:, q, 0, :], w_pairs[:, :, 0:P, :], nc.scalar.copy)
-            transpose_rows(rows[:, q, 1, :], w_pairs[:, :, P : 2 * P, :], nc.vector.tensor_copy)
+            transpose_rows(w_sorted[:, 0, :, :], w_pairs[:, :, 0:P, :], nc.scalar.copy)
+            transpose_rows(w_sorted[:, 1, :, :], w_pairs[:, :, P : 2 * P, :], second_copy)
             cols = slice(2 * P * q, 2 * P * (q + 1))
             for c in range(PASSES):
                 nc.vector.quantize_mx(
@@ -184,6 +187,11 @@ def tile_localattention_pb_kernel(tc, x, Wv, bv, attn_band, Wo, bo, out):
                     scales=scales[:, c, cols],
                     in_=w_pairs[:, c, :, :].rearrange("p n u -> p (n u)").bitcast(BF16),
                 )
+
+        def sort_pair(rows, q, copy):
+            return sort_words(
+                rows[:, q, :, :].rearrange("p e k -> p (e k)").bitcast(F32), 2, copy
+            )
 
         wv_tiles = weight_tiles("wv")
         wo_tiles = weight_tiles("wo")
@@ -205,22 +213,19 @@ def tile_localattention_pb_kernel(tc, x, Wv, bv, attn_band, Wo, bo, out):
         bv_all = keep.tile([P, FEATURES], F32)
         bo_all = keep.tile([P, FEATURES], F32)
 
-        def spread_biases():
-            for half in range(HALVES):
-                cols = slice(half * N_TILE, (half + 1) * N_TILE)
-                bv_acc = psum.tile([P, N_TILE], F32, tag="acc")
-                nc.tensor.matmul(
-                    out=bv_acc[:], lhsT=ones[:], rhs=bias_rows["bv"][:, cols], start=True, stop=True
-                )
+        def spread(label, half):
+            acc = psum.tile([P, N_TILE], F32, tag="acc")
+            cols = slice(half * N_TILE, (half + 1) * N_TILE)
+            nc.tensor.matmul(
+                out=acc[:], lhsT=ones[:], rhs=bias_rows[label][:, cols], start=True, stop=True
+            )
+            if label == "bo":
+                nc.scalar.copy(out=bo_all[:, cols], in_=acc[:])
+            else:
                 nc.scalar.copy(
                     out=bv_all[:, cols].rearrange("p (t m) -> p t m", t=PACK),
-                    in_=bv_acc[:].rearrange("p (m t) -> p t m", t=PACK),
+                    in_=acc[:].rearrange("p (m t) -> p t m", t=PACK),
                 )
-                bo_acc = psum.tile([P, N_TILE], F32, tag="acc")
-                nc.tensor.matmul(
-                    out=bo_acc[:], lhsT=ones[:], rhs=bias_rows["bo"][:, cols], start=True, stop=True
-                )
-                nc.scalar.copy(out=bo_all[:, cols], in_=bo_acc[:])
 
         v_rows = {}
 
@@ -291,8 +296,10 @@ def tile_localattention_pb_kernel(tc, x, Wv, bv, attn_band, Wo, bo, out):
 
         prepare_x(0)
         for q in range(ROW_PAIRS):
-            prepare_weight_pair(wv_rows, wv_tiles, q)
-        spread_biases()
+            wv_sorted = sort_pair(wv_rows, q, nc.vector.tensor_copy)
+            prepare_weight_pair(wv_sorted, wv_tiles, q, nc.scalar.copy)
+        for half in range(HALVES):
+            spread("bv", half)
         for w in range(1, ROUND):
             prepare_x(w)
         for first_w in range(0, N_WINDOWS, ROUND):
@@ -302,14 +309,21 @@ def tile_localattention_pb_kernel(tc, x, Wv, bv, attn_band, Wo, bo, out):
                 transpose_band()
             for w in range(first_w, min(first_w + ROUND, N_WINDOWS)):
                 project_v(w)
+        for half in range(HALVES):
+            spread("bo", half)
 
+        wo_sorted = {0: sort_pair(wo_rows, 0, nc.scalar.copy)}
+        projected = 0
         for w in range(N_WINDOWS + 1):
+            if w + 1 < ROW_PAIRS:
+                wo_sorted[w + 1] = sort_pair(wo_rows, w + 1, nc.scalar.copy)
             if w < N_WINDOWS:
                 mix(w)
-            if w >= 2:
-                project_out(w - 2)
-            if w < HALVES:
-                for q in range(w * PAIRS_PER_HALF, (w + 1) * PAIRS_PER_HALF):
-                    prepare_weight_pair(wo_rows, wo_tiles, q)
+            if w < ROW_PAIRS:
+                prepare_weight_pair(wo_sorted[w], wo_tiles, w, nc.vector.tensor_copy)
+            else:
+                for tb in range(projected, min(w - 1, projected + 2)):
+                    project_out(tb)
+                projected = min(w - 1, projected + 2)
             if 1 <= w < N_WINDOWS:
                 quantise_ctx(w - 1)

@@ -31,6 +31,7 @@ assert (SEAM_WINDOW - 1) * WIN_STEP + P <= SEQ and SEAM == P // 2
 ROW_PITCH = 136
 
 ROUND = 2
+N_ROUNDS = (N_WINDOWS + ROUND - 1) // ROUND
 
 FLOPS = 2 * 2 * TOKENS * FEATURES * FEATURES + 2 * TOKENS * TAPS * FEATURES
 
@@ -52,7 +53,7 @@ def tile_localattention_pb_kernel(tc, x, Wv, bv, attn_band, Wo, bo, out):
     with ExitStack() as stack:
         keep = stack.enter_context(tc.tile_pool(name="keep", bufs=1))
         x_pool = stack.enter_context(tc.tile_pool(name="x_pool", bufs=N_WINDOWS))
-        sorted_pool = stack.enter_context(tc.tile_pool(name="sorted_pool", bufs=2))
+        sorted_pool = stack.enter_context(tc.tile_pool(name="sorted_pool", bufs=4))
         pairs_pool = stack.enter_context(tc.tile_pool(name="pairs_pool", bufs=3))
         v_pool = stack.enter_context(tc.tile_pool(name="v_pool", bufs=N_WINDOWS))
         out_pool = stack.enter_context(tc.tile_pool(name="out_pool", bufs=4))
@@ -144,26 +145,35 @@ def tile_localattention_pb_kernel(tc, x, Wv, bv, attn_band, Wo, bo, out):
                 nc.scalar.copy(out=band_t[:, w0 : w0 + count, :], in_=flipped[:, 0:count, :])
 
         def sort_words(words, count, copy):
-            sorted_words = sorted_pool.tile([P, count, PACK, P], F32, tag="sorted" + str(count))
+            sorted_words = sorted_pool.tile([P, count, PASSES, 2, P], F32, tag="sorted" + str(count))
             copy(
-                out=sorted_words[:].rearrange("p n (c u) i -> p (n c) u i", u=2),
+                out=sorted_words[:].rearrange("p n c u i -> p (n c) u i"),
                 in_=words.rearrange("p (n i u) -> p n u i", i=P, u=2),
             )
             return sorted_words
 
+        def unsorted(rows):
+            return rows.bitcast(F32).rearrange("p (c i u) -> p c u i", c=PASSES, u=2)
+
         def transpose_rows(words, pairs, copy):
             flipped = psum.tile([P, PACK, P], F32, tag="flipped")
-            for j in range(PACK):
-                nc.tensor.transpose(flipped[:, j, :], words[:, j, :], ident[:])
+            for c in range(PASSES):
+                for u in range(2):
+                    nc.tensor.transpose(flipped[:, 2 * c + u, :], words[:, c, u, :], ident[:])
             copy(out=pairs, in_=flipped[:].rearrange("p (c u) r -> p c r u", u=2))
 
         x_codes = keep.tile([P, N_WINDOWS, PASSES, P], U32, align_bytes=64)
         x_scales = keep.tile([P, N_WINDOWS, PASSES, P], U8, align_bytes=64)
 
+        x_words = {}
+
+        def sort_x(w):
+            x_sorted = sort_words(x_rows[w][:].bitcast(F32), 1, nc.scalar.copy)
+            x_words[w] = x_sorted[:, 0, :, :, :]
+
         def prepare_x(w):
             x_pairs = pairs_pool.tile([P, PASSES, P, 2], F32, align_bytes=64)
-            x_sorted = sort_words(x_rows[w][:].bitcast(F32), 1, nc.scalar.copy)
-            transpose_rows(x_sorted[:, 0, :, :], x_pairs[:], nc.scalar.copy)
+            transpose_rows(x_words[w], x_pairs[:], nc.scalar.copy)
             nc.vector.quantize_mx(
                 out=x_codes[:, w, :, :].rearrange("p c r -> p (c r)").bitcast(FP8X4),
                 scales=x_scales[:, w, :, :].rearrange("p c r -> p (c r)"),
@@ -175,11 +185,11 @@ def tile_localattention_pb_kernel(tc, x, Wv, bv, attn_band, Wo, bo, out):
             scales = keep.tile([P, PASSES, FEATURES], U8, name=label + "_scales", align_bytes=64)
             return codes, scales
 
-        def prepare_weight_pair(w_sorted, tiles, q, second_copy):
+        def prepare_weight_pair(words, tiles, q, second_copy):
             codes, scales = tiles
             w_pairs = pairs_pool.tile([P, PASSES, 2 * P, 2], F32, align_bytes=64)
-            transpose_rows(w_sorted[:, 0, :, :], w_pairs[:, :, 0:P, :], nc.scalar.copy)
-            transpose_rows(w_sorted[:, 1, :, :], w_pairs[:, :, P : 2 * P, :], second_copy)
+            transpose_rows(words[0], w_pairs[:, :, 0:P, :], nc.scalar.copy)
+            transpose_rows(words[1], w_pairs[:, :, P : 2 * P, :], second_copy)
             cols = slice(2 * P * q, 2 * P * (q + 1))
             for c in range(PASSES):
                 nc.vector.quantize_mx(
@@ -188,10 +198,13 @@ def tile_localattention_pb_kernel(tc, x, Wv, bv, attn_band, Wo, bo, out):
                     in_=w_pairs[:, c, :, :].rearrange("p n u -> p (n u)").bitcast(BF16),
                 )
 
-        def sort_pair(rows, q, copy):
-            return sort_words(
-                rows[:, q, :, :].rearrange("p e k -> p (e k)").bitcast(F32), 2, copy
+        wo_words = {}
+
+        def sort_wo(q):
+            wo_sorted = sort_words(
+                wo_rows[:, q, :, :].rearrange("p j k -> p (j k)").bitcast(F32), 2, nc.scalar.copy
             )
+            wo_words[q] = [wo_sorted[:, j, :, :, :] for j in range(2)]
 
         wv_tiles = weight_tiles("wv")
         wo_tiles = weight_tiles("wo")
@@ -294,33 +307,41 @@ def tile_localattention_pb_kernel(tc, x, Wv, bv, attn_band, Wo, bo, out):
                 nc.vector.tensor_tensor(out=out_sb[:], in0=out_acc[:], in1=bo_all[:, cols], op=ADD)
                 nc.sync.dma_start(out=out_hbm[tokens, cols], in_=out_sb[:])
 
+        for w in range(2 * ROUND):
+            x_words[w] = unsorted(x_rows[w][:])
         prepare_x(0)
         for q in range(ROW_PAIRS):
-            wv_sorted = sort_pair(wv_rows, q, nc.vector.tensor_copy)
-            prepare_weight_pair(wv_sorted, wv_tiles, q, nc.scalar.copy)
-        for half in range(HALVES):
-            spread("bv", half)
+            wv_words = [unsorted(wv_rows[:, q, e, :]) for e in range(2)]
+            prepare_weight_pair(wv_words, wv_tiles, q, nc.vector.tensor_copy)
         for w in range(1, ROUND):
             prepare_x(w)
-        for first_w in range(0, N_WINDOWS, ROUND):
-            for w in range(first_w + ROUND, min(first_w + 2 * ROUND, N_WINDOWS)):
+        for half in range(HALVES):
+            spread("bv", half)
+        wo_sorted = 0
+        for r in range(N_ROUNDS):
+            for w in range((r + 1) * ROUND, min((r + 2) * ROUND, N_WINDOWS)):
                 prepare_x(w)
-            if first_w + ROUND >= N_WINDOWS:
+            for w in range((r + 2) * ROUND, min((r + 3) * ROUND, N_WINDOWS)):
+                sort_x(w)
+            if r == N_ROUNDS - 1:
                 transpose_band()
-            for w in range(first_w, min(first_w + ROUND, N_WINDOWS)):
+            elif r >= N_ROUNDS - 3:
+                for q in range(wo_sorted, r - (N_ROUNDS - 3) + 1 + wo_sorted):
+                    sort_wo(q)
+                wo_sorted += r - (N_ROUNDS - 3) + 1
+            for w in range(r * ROUND, min((r + 1) * ROUND, N_WINDOWS)):
                 project_v(w)
+        for q in range(wo_sorted, ROW_PAIRS):
+            sort_wo(q)
         for half in range(HALVES):
             spread("bo", half)
 
-        wo_sorted = {0: sort_pair(wo_rows, 0, nc.scalar.copy)}
         projected = 0
         for w in range(N_WINDOWS + 1):
-            if w + 1 < ROW_PAIRS:
-                wo_sorted[w + 1] = sort_pair(wo_rows, w + 1, nc.scalar.copy)
             if w < N_WINDOWS:
                 mix(w)
             if w < ROW_PAIRS:
-                prepare_weight_pair(wo_sorted[w], wo_tiles, w, nc.vector.tensor_copy)
+                prepare_weight_pair(wo_words[w], wo_tiles, w, nc.scalar.copy)
             else:
                 for tb in range(projected, min(w - 1, projected + 2)):
                     project_out(tb)

@@ -63,38 +63,15 @@ def tile_localattention_pb_kernel(tc, x, Wv, bv, attn_band, Wo, bo, out):
         ident = keep.tile([P, P], F32)
         make_identity(nc, ident[:])
 
+        bv_row = keep.tile([P, FEATURES], BF16)
+        nc.vector.memset(bv_row[:].bitcast(mybir.dt.int32), 0)
+        ones = keep.tile([P, P], BF16)
+        nc.vector.memset(ones[:], 1.0)
+
         table_in = keep.tile([P, 1], F32)
         nc.vector.memset(table_in[:], 0.0)
         table_out = keep.tile([P, 1], F32)
         nc.scalar.copy(out=table_out[:], in_=table_in[:])
-
-        ones = keep.tile([P, P], BF16)
-        nc.vector.memset(ones[:], 1.0)
-        bias_rows = {}
-        for label, bias in (("bv", bv), ("bo", bo)):
-            bias_row = keep.tile([P, FEATURES], BF16, name=label + "_row")
-            nc.vector.memset(bias_row[:].bitcast(mybir.dt.int32), 0)
-            nc.scalar.dma_start(out=bias_row[0:1, :], in_=bias.rearrange("(o n) -> o n", o=1))
-            bias_rows[label] = bias_row
-
-        taps_win = keep.tile([P, N_WINDOWS, TAP_SLOT], BF16)
-        nc.scalar.dma_start(
-            out=taps_win[0:WIN_STEP, :, 0:TAPS],
-            in_=taps_hbm[0 : N_WINDOWS * WIN_STEP, :].rearrange("(w r) o -> r w o", r=WIN_STEP),
-        )
-        nc.scalar.dma_start(
-            out=taps_win[WIN_STEP:P, :, 0:TAPS],
-            in_=taps_hbm[P - WIN_STEP : TOKENS, :].rearrange("(w r) o -> r w o", r=WIN_STEP)[
-                2 * WIN_STEP - P : WIN_STEP
-            ],
-        )
-
-        padded = keep.tile([P, N_WINDOWS, ROW_PITCH], F32)
-        nc.gpsimd.memset(padded[:], 0.0)
-        nc.gpsimd.tensor_copy(out=padded[:, :, 0:TAPS], in_=taps_win[:, :, 0:TAPS])
-        nc.gpsimd.dma_start(
-            out=parked.rearrange("(w p q) -> p w q", p=P, q=ROW_PITCH), in_=padded[:]
-        )
 
         x_rows = {}
 
@@ -114,6 +91,27 @@ def tile_localattention_pb_kernel(tc, x, Wv, bv, attn_band, Wo, bo, out):
                     "(m t) k -> m t k", t=PACK
                 )[:, 2 * upper : 2 * upper + 2, :],
             )
+            if q == 0:
+                nc.sync.dma_start(out=bv_row[0:1, :], in_=bv.rearrange("(o n) -> o n", o=1))
+        taps_win = keep.tile([P, N_WINDOWS, TAP_SLOT], BF16)
+        nc.sync.dma_start(
+            out=taps_win[0:WIN_STEP, :, 0:TAPS],
+            in_=taps_hbm[0 : N_WINDOWS * WIN_STEP, :].rearrange("(w r) o -> r w o", r=WIN_STEP),
+        )
+        nc.sync.dma_start(
+            out=taps_win[WIN_STEP:P, :, 0:TAPS],
+            in_=taps_hbm[P - WIN_STEP : TOKENS, :].rearrange("(w r) o -> r w o", r=WIN_STEP)[
+                2 * WIN_STEP - P : WIN_STEP
+            ],
+        )
+
+        padded = keep.tile([P, N_WINDOWS, ROW_PITCH], F32)
+        nc.gpsimd.memset(padded[:], 0.0)
+        nc.gpsimd.tensor_copy(out=padded[:, :, 0:TAPS], in_=taps_win[:, :, 0:TAPS])
+        nc.gpsimd.dma_start(
+            out=parked.rearrange("(w p q) -> p w q", p=P, q=ROW_PITCH), in_=padded[:]
+        )
+
         for w in range(1, N_WINDOWS):
             load_x(w)
 
@@ -133,6 +131,9 @@ def tile_localattention_pb_kernel(tc, x, Wv, bv, attn_band, Wo, bo, out):
         )
         nc.gpsimd.memset(band[0:SEAM, SEAM_WINDOW, SEAM:P], 0.0)
         nc.gpsimd.memset(band[SEAM:P, SEAM_WINDOW, 0:SEAM], 0.0)
+
+        bo_all = keep.tile([P, FEATURES], BF16)
+        nc.sync.dma_start(out=bo_all[:], in_=bo.partition_broadcast(P))
 
         band_t = keep.tile([P, N_WINDOWS, P], F32)
 
@@ -209,32 +210,35 @@ def tile_localattention_pb_kernel(tc, x, Wv, bv, attn_band, Wo, bo, out):
         wv_tiles = weight_tiles("wv")
         wo_tiles = weight_tiles("wo")
 
-        def product(acc, left_codes, left_scales, tiles, half):
+        def product(left_codes, left_scales, tiles):
             codes, scales = tiles
-            cols = slice(half * N_TILE, (half + 1) * N_TILE)
+            accs = []
+            for half in range(HALVES):
+                acc = psum.tile([P, N_TILE], F32, tag="acc")
+                accs.append(acc)
             for c in range(PASSES):
-                nc.tensor.matmul_mx(
-                    out=acc,
-                    lhsT=left_codes[c].bitcast(FP8X4),
-                    lhsT_scale=left_scales[c],
-                    rhs=codes[:, c, cols].bitcast(FP8X4),
-                    rhs_scale=scales[:, c, cols],
-                    start=(c == 0),
-                    stop=(c == PASSES - 1),
+                for half in range(HALVES):
+                    cols = slice(half * N_TILE, (half + 1) * N_TILE)
+                    nc.tensor.matmul_mx(
+                        out=accs[half][:],
+                        lhsT=left_codes[c].bitcast(FP8X4),
+                        lhsT_scale=left_scales[c],
+                        rhs=codes[:, c, cols].bitcast(FP8X4),
+                        rhs_scale=scales[:, c, cols],
+                        start=(c == 0),
+                        stop=(c == PASSES - 1),
+                    )
+            return accs
+
+        bv_all = keep.tile([P, FEATURES], BF16)
+
+        def spread_bv():
+            for half in range(HALVES):
+                acc = psum.tile([P, N_TILE], F32, tag="acc")
+                cols = slice(half * N_TILE, (half + 1) * N_TILE)
+                nc.tensor.matmul(
+                    out=acc[:], lhsT=ones[:], rhs=bv_row[:, cols], start=True, stop=True
                 )
-
-        bv_all = keep.tile([P, FEATURES], F32)
-        bo_all = keep.tile([P, FEATURES], F32)
-
-        def spread(label, half):
-            acc = psum.tile([P, N_TILE], F32, tag="acc")
-            cols = slice(half * N_TILE, (half + 1) * N_TILE)
-            nc.tensor.matmul(
-                out=acc[:], lhsT=ones[:], rhs=bias_rows[label][:, cols], start=True, stop=True
-            )
-            if label == "bo":
-                nc.scalar.copy(out=bo_all[:, cols], in_=acc[:])
-            else:
                 nc.scalar.copy(
                     out=bv_all[:, cols].rearrange("p (t m) -> p t m", t=PACK),
                     in_=acc[:].rearrange("p (m t) -> p t m", t=PACK),
@@ -243,19 +247,16 @@ def tile_localattention_pb_kernel(tc, x, Wv, bv, attn_band, Wo, bo, out):
         v_rows = {}
 
         def project_v(w):
+            v_accs = product(
+                [x_codes[:, w, c, :] for c in range(PASSES)],
+                [x_scales[:, w, c, :] for c in range(PASSES)],
+                wv_tiles,
+            )
             v_win = v_pool.tile([P, FEATURES], F32)
             for half in range(HALVES):
                 cols = slice(half * N_TILE, (half + 1) * N_TILE)
-                v_acc = psum.tile([P, N_TILE], F32, tag="acc")
-                product(
-                    v_acc[:],
-                    [x_codes[:, w, c, :] for c in range(PASSES)],
-                    [x_scales[:, w, c, :] for c in range(PASSES)],
-                    wv_tiles,
-                    half,
-                )
                 nc.vector.tensor_tensor(
-                    out=v_win[:, cols], in0=v_acc[:], in1=bv_all[:, cols], op=ADD
+                    out=v_win[:, cols], in0=v_accs[half][:], in1=bv_all[:, cols], op=ADD
                 )
             v_rows[w] = v_win
 
@@ -263,24 +264,23 @@ def tile_localattention_pb_kernel(tc, x, Wv, bv, attn_band, Wo, bo, out):
         ctx_codes = keep.tile([P, PASSES, TOKENS], U32, align_bytes=64)
         ctx_scales = keep.tile([P, PASSES, TOKENS], U8, align_bytes=64)
 
-        def mix(w):
+        def mix(w, c):
             first, lo, hi = window_place(w)
-            for c in range(PASSES):
-                mixed = psum.tile([P, PACK, P], F32, tag="flipped")
-                for t in range(PACK):
-                    blk = c * PACK + t
-                    nc.tensor.matmul(
-                        out=mixed[:, t, lo:hi],
-                        lhsT=v_rows[w][:, blk * P : (blk + 1) * P],
-                        rhs=band_t[:, w, lo:hi],
-                        start=True,
-                        stop=True,
-                    )
-                copy = nc.scalar.copy if c == 0 else nc.vector.tensor_copy
-                copy(
-                    out=ctx_quads[:, c, first + lo : first + hi, :],
-                    in_=mixed[:, :, lo:hi].rearrange("p t i -> p i t"),
+            mixed = psum.tile([P, PACK, P], F32, tag="flipped")
+            for t in range(PACK):
+                blk = c * PACK + t
+                nc.tensor.matmul(
+                    out=mixed[:, t, lo:hi],
+                    lhsT=v_rows[w][:, blk * P : (blk + 1) * P],
+                    rhs=band_t[:, w, lo:hi],
+                    start=True,
+                    stop=True,
                 )
+            copy = nc.scalar.copy if (c == 0) == (w < ROW_PAIRS) else nc.vector.tensor_copy
+            copy(
+                out=ctx_quads[:, c, first + lo : first + hi, :],
+                in_=mixed[:, :, lo:hi].rearrange("p t i -> p i t"),
+            )
 
         def quantise_ctx(tb):
             tokens = slice(tb * P, (tb + 1) * P)
@@ -293,18 +293,17 @@ def tile_localattention_pb_kernel(tc, x, Wv, bv, attn_band, Wo, bo, out):
 
         def project_out(tb):
             tokens = slice(tb * P, (tb + 1) * P)
+            out_accs = product(
+                [ctx_codes[:, c, tokens] for c in range(PASSES)],
+                [ctx_scales[:, c, tokens] for c in range(PASSES)],
+                wo_tiles,
+            )
             for half in range(HALVES):
                 cols = slice(half * N_TILE, (half + 1) * N_TILE)
-                out_acc = psum.tile([P, N_TILE], F32, tag="acc")
-                product(
-                    out_acc[:],
-                    [ctx_codes[:, c, tokens] for c in range(PASSES)],
-                    [ctx_scales[:, c, tokens] for c in range(PASSES)],
-                    wo_tiles,
-                    half,
-                )
                 out_sb = out_pool.tile([P, N_TILE], F32)
-                nc.vector.tensor_tensor(out=out_sb[:], in0=out_acc[:], in1=bo_all[:, cols], op=ADD)
+                nc.vector.tensor_tensor(
+                    out=out_sb[:], in0=out_accs[half][:], in1=bo_all[:, cols], op=ADD
+                )
                 nc.sync.dma_start(out=out_hbm[tokens, cols], in_=out_sb[:])
 
         for w in range(2 * ROUND):
@@ -313,10 +312,10 @@ def tile_localattention_pb_kernel(tc, x, Wv, bv, attn_band, Wo, bo, out):
         for q in range(ROW_PAIRS):
             wv_words = [unsorted(wv_rows[:, q, e, :]) for e in range(2)]
             prepare_weight_pair(wv_words, wv_tiles, q, nc.vector.tensor_copy)
+            if q == 0:
+                spread_bv()
         for w in range(1, ROUND):
             prepare_x(w)
-        for half in range(HALVES):
-            spread("bv", half)
         wo_sorted = 0
         for r in range(N_ROUNDS):
             for w in range((r + 1) * ROUND, min((r + 2) * ROUND, N_WINDOWS)):
@@ -333,18 +332,17 @@ def tile_localattention_pb_kernel(tc, x, Wv, bv, attn_band, Wo, bo, out):
                 project_v(w)
         for q in range(wo_sorted, ROW_PAIRS):
             sort_wo(q)
-        for half in range(HALVES):
-            spread("bo", half)
 
         projected = 0
-        for w in range(N_WINDOWS + 1):
-            if w < N_WINDOWS:
-                mix(w)
+        for w in range(N_WINDOWS):
+            for c in range(PASSES):
+                mix(w, c)
             if w < ROW_PAIRS:
                 prepare_weight_pair(wo_words[w], wo_tiles, w, nc.scalar.copy)
-            else:
+            if w >= 1:
+                quantise_ctx(w - 1)
+            if w >= ROW_PAIRS:
                 for tb in range(projected, min(w - 1, projected + 2)):
                     project_out(tb)
                 projected = min(w - 1, projected + 2)
-            if 1 <= w < N_WINDOWS:
-                quantise_ctx(w - 1)
+        project_out(projected)

@@ -14,6 +14,7 @@ P = 128
 PACK = 4
 BATCH, SEQ, FEATURES = 2, 512, 1024
 TOKENS = BATCH * SEQ
+BLOCKS = TOKENS // 128
 TAPS, HALF = 11, 5
 TAP_SLOT = 16
 PASSES = FEATURES // (P * PACK)
@@ -31,7 +32,7 @@ assert (SEAM_WINDOW - 1) * WIN_STEP + P <= SEQ and SEAM == P // 2
 ROW_PITCH = 136
 
 ROUND = 2
-N_ROUNDS = (N_WINDOWS + ROUND - 1) // ROUND
+N_ROUNDS = BLOCKS // ROUND
 
 FLOPS = 2 * 2 * TOKENS * FEATURES * FEATURES + 2 * TOKENS * TAPS * FEATURES
 
@@ -52,8 +53,9 @@ def tile_localattention_pb_kernel(tc, x, Wv, bv, attn_band, Wo, bo, out):
 
     with ExitStack() as stack:
         keep = stack.enter_context(tc.tile_pool(name="keep", bufs=1))
-        x_pool = stack.enter_context(tc.tile_pool(name="x_pool", bufs=N_WINDOWS))
+        x_pool = stack.enter_context(tc.tile_pool(name="x_pool", bufs=BLOCKS))
         sorted_pool = stack.enter_context(tc.tile_pool(name="sorted_pool", bufs=4))
+        x_pairs_pool = stack.enter_context(tc.tile_pool(name="x_pairs_pool", bufs=4))
         pairs_pool = stack.enter_context(tc.tile_pool(name="pairs_pool", bufs=3))
         v_pool = stack.enter_context(tc.tile_pool(name="v_pool", bufs=N_WINDOWS))
         out_pool = stack.enter_context(tc.tile_pool(name="out_pool", bufs=4))
@@ -75,22 +77,22 @@ def tile_localattention_pb_kernel(tc, x, Wv, bv, attn_band, Wo, bo, out):
 
         x_rows = {}
 
-        def load_x(w):
-            first, lo, hi = window_place(w)
-            x_win = x_pool.tile([P, FEATURES], BF16)
-            nc.sync.dma_start(out=x_win[:], in_=x_hbm[first : first + P, :])
-            x_rows[w] = x_win
+        def load_x(b):
+            x_block = x_pool.tile([P, FEATURES], BF16)
+            nc.sync.dma_start(out=x_block[:], in_=x_hbm[b * P : (b + 1) * P, :])
+            x_rows[b] = x_block
 
         load_x(0)
         wv_rows = keep.tile([P, ROW_PAIRS, 2, FEATURES], BF16)
         for q in range(ROW_PAIRS):
             group, upper = divmod(q, 2)
-            nc.sync.dma_start(
-                out=wv_rows[:, q, :, :],
-                in_=Wv[PACK * P * group : PACK * P * (group + 1), :].rearrange(
-                    "(m t) k -> m t k", t=PACK
-                )[:, 2 * upper : 2 * upper + 2, :],
+            rows_of_group = Wv[PACK * P * group : PACK * P * (group + 1), :].rearrange(
+                "(m t) k -> m t k", t=PACK
             )
+            for e in range(2):
+                nc.sync.dma_start(
+                    out=wv_rows[:, q, e, :], in_=rows_of_group[:, 2 * upper + e, :]
+                )
             if q == 0:
                 nc.sync.dma_start(out=bv_row[0:1, :], in_=bv.rearrange("(o n) -> o n", o=1))
         taps_win = keep.tile([P, N_WINDOWS, TAP_SLOT], BF16)
@@ -112,15 +114,8 @@ def tile_localattention_pb_kernel(tc, x, Wv, bv, attn_band, Wo, bo, out):
             out=parked.rearrange("(w p q) -> p w q", p=P, q=ROW_PITCH), in_=padded[:]
         )
 
-        for w in range(1, N_WINDOWS):
-            load_x(w)
-
-        wo_rows = keep.tile([P, ROW_PAIRS, 2, FEATURES], BF16)
-        for q in range(ROW_PAIRS):
-            nc.sync.dma_start(
-                out=wo_rows[:, q, :, :],
-                in_=Wo[2 * P * q : 2 * P * (q + 1), :].rearrange("(j m) k -> m j k", m=P),
-            )
+        for b in range(1, BLOCKS):
+            load_x(b)
 
         band = keep.tile([P, N_WINDOWS, P], F32)
         nc.sync.dma_start(
@@ -131,6 +126,13 @@ def tile_localattention_pb_kernel(tc, x, Wv, bv, attn_band, Wo, bo, out):
         )
         nc.gpsimd.memset(band[0:SEAM, SEAM_WINDOW, SEAM:P], 0.0)
         nc.gpsimd.memset(band[SEAM:P, SEAM_WINDOW, 0:SEAM], 0.0)
+
+        wo_rows = keep.tile([P, ROW_PAIRS, 2, FEATURES], BF16)
+        for q in range(ROW_PAIRS):
+            nc.sync.dma_start(
+                out=wo_rows[:, q, :, :],
+                in_=Wo[2 * P * q : 2 * P * (q + 1), :].rearrange("(j m) k -> m j k", m=P),
+            )
 
         bo_all = keep.tile([P, FEATURES], BF16)
         nc.sync.dma_start(out=bo_all[:], in_=bo.partition_broadcast(P))
@@ -156,30 +158,44 @@ def tile_localattention_pb_kernel(tc, x, Wv, bv, attn_band, Wo, bo, out):
         def unsorted(rows):
             return rows.bitcast(F32).rearrange("p (c i u) -> p c u i", c=PASSES, u=2)
 
-        def transpose_rows(words, pairs, copy):
+        def transpose_rows(words):
             flipped = psum.tile([P, PACK, P], F32, tag="flipped")
             for c in range(PASSES):
                 for u in range(2):
                     nc.tensor.transpose(flipped[:, 2 * c + u, :], words[:, c, u, :], ident[:])
-            copy(out=pairs, in_=flipped[:].rearrange("p (c u) r -> p c r u", u=2))
+            return flipped[:].rearrange("p (c u) r -> p c r u", u=2)
 
         x_codes = keep.tile([P, N_WINDOWS, PASSES, P], U32, align_bytes=64)
         x_scales = keep.tile([P, N_WINDOWS, PASSES, P], U8, align_bytes=64)
 
         x_words = {}
 
-        def sort_x(w):
-            x_sorted = sort_words(x_rows[w][:].bitcast(F32), 1, nc.scalar.copy)
-            x_words[w] = x_sorted[:, 0, :, :, :]
+        def sort_x(b):
+            x_sorted = sort_words(x_rows[b][:].bitcast(F32), 1, nc.scalar.copy)
+            x_words[b] = x_sorted[:, 0, :, :, :]
 
-        def prepare_x(w):
-            x_pairs = pairs_pool.tile([P, PASSES, P, 2], F32, align_bytes=64)
-            transpose_rows(x_words[w], x_pairs[:], nc.scalar.copy)
-            nc.vector.quantize_mx(
-                out=x_codes[:, w, :, :].rearrange("p c r -> p (c r)").bitcast(FP8X4),
-                scales=x_scales[:, w, :, :].rearrange("p c r -> p (c r)"),
-                in_=x_pairs[:].rearrange("p c r u -> p (c r u)").bitcast(BF16),
-            )
+        x_pairs_of = {}
+
+        def prepare_x(b):
+            flipped_pairs = transpose_rows(x_words[b])
+            for w in range(N_WINDOWS):
+                first = w * WIN_STEP
+                start, stop = max(b * P, first), min((b + 1) * P, first + P)
+                if start >= stop:
+                    continue
+                if w not in x_pairs_of:
+                    x_pairs = x_pairs_pool.tile([P, PASSES, P, 2], F32, align_bytes=64)
+                    x_pairs_of[w] = x_pairs
+                nc.scalar.copy(
+                    out=x_pairs_of[w][:, :, start - first : stop - first, :],
+                    in_=flipped_pairs[:, :, start - b * P : stop - b * P, :],
+                )
+                if stop == first + P:
+                    nc.vector.quantize_mx(
+                        out=x_codes[:, w, :, :].rearrange("p c r -> p (c r)").bitcast(FP8X4),
+                        scales=x_scales[:, w, :, :].rearrange("p c r -> p (c r)"),
+                        in_=x_pairs_of[w][:].rearrange("p c r u -> p (c r u)").bitcast(BF16),
+                    )
 
         def weight_tiles(label):
             codes = keep.tile([P, PASSES, FEATURES], U32, name=label + "_codes", align_bytes=64)
@@ -189,8 +205,8 @@ def tile_localattention_pb_kernel(tc, x, Wv, bv, attn_band, Wo, bo, out):
         def prepare_weight_pair(words, tiles, q, second_copy):
             codes, scales = tiles
             w_pairs = pairs_pool.tile([P, PASSES, 2 * P, 2], F32, align_bytes=64)
-            transpose_rows(words[0], w_pairs[:, :, 0:P, :], nc.scalar.copy)
-            transpose_rows(words[1], w_pairs[:, :, P : 2 * P, :], second_copy)
+            nc.scalar.copy(out=w_pairs[:, :, 0:P, :], in_=transpose_rows(words[0]))
+            second_copy(out=w_pairs[:, :, P : 2 * P, :], in_=transpose_rows(words[1]))
             cols = slice(2 * P * q, 2 * P * (q + 1))
             for c in range(PASSES):
                 nc.vector.quantize_mx(
@@ -298,37 +314,42 @@ def tile_localattention_pb_kernel(tc, x, Wv, bv, attn_band, Wo, bo, out):
                 [ctx_scales[:, c, tokens] for c in range(PASSES)],
                 wo_tiles,
             )
-            for half in range(HALVES):
-                cols = slice(half * N_TILE, (half + 1) * N_TILE)
-                out_sb = out_pool.tile([P, N_TILE], F32)
+            width = N_TILE // 2 if tb == BLOCKS - 1 else N_TILE
+            for start in range(0, FEATURES, width):
+                cols = slice(start, start + width)
+                half, offset = divmod(start, N_TILE)
+                out_sb = out_pool.tile([P, width], F32, tag="out" + str(width))
                 nc.vector.tensor_tensor(
-                    out=out_sb[:], in0=out_accs[half][:], in1=bo_all[:, cols], op=ADD
+                    out=out_sb[:],
+                    in0=out_accs[half][:, offset : offset + width],
+                    in1=bo_all[:, cols],
+                    op=ADD,
                 )
                 nc.sync.dma_start(out=out_hbm[tokens, cols], in_=out_sb[:])
 
-        for w in range(2 * ROUND):
-            x_words[w] = unsorted(x_rows[w][:])
+        for b in range(2 * ROUND):
+            x_words[b] = unsorted(x_rows[b][:])
         prepare_x(0)
         for q in range(ROW_PAIRS):
             wv_words = [unsorted(wv_rows[:, q, e, :]) for e in range(2)]
             prepare_weight_pair(wv_words, wv_tiles, q, nc.vector.tensor_copy)
             if q == 0:
                 spread_bv()
-        for w in range(1, ROUND):
-            prepare_x(w)
+        for b in range(1, ROUND):
+            prepare_x(b)
         wo_sorted = 0
         for r in range(N_ROUNDS):
-            for w in range((r + 1) * ROUND, min((r + 2) * ROUND, N_WINDOWS)):
-                prepare_x(w)
-            for w in range((r + 2) * ROUND, min((r + 3) * ROUND, N_WINDOWS)):
-                sort_x(w)
+            for b in range((r + 1) * ROUND, min((r + 2) * ROUND, BLOCKS)):
+                prepare_x(b)
+            for b in range((r + 2) * ROUND, min((r + 3) * ROUND, BLOCKS)):
+                sort_x(b)
             if r == N_ROUNDS - 1:
                 transpose_band()
-            elif r >= N_ROUNDS - 3:
-                for q in range(wo_sorted, r - (N_ROUNDS - 3) + 1 + wo_sorted):
+            if r >= N_ROUNDS - 2:
+                for q in range(wo_sorted, r - (N_ROUNDS - 2) + 1 + wo_sorted):
                     sort_wo(q)
-                wo_sorted += r - (N_ROUNDS - 3) + 1
-            for w in range(r * ROUND, min((r + 1) * ROUND, N_WINDOWS)):
+                wo_sorted += r - (N_ROUNDS - 2) + 1
+            for w in range(r * ROUND, (r + 1) * ROUND if r < N_ROUNDS - 1 else N_WINDOWS):
                 project_v(w)
         for q in range(wo_sorted, ROW_PAIRS):
             sort_wo(q)

from contextlib import ExitStack

import concourse.mybir as mybir
from concourse.masks import make_identity

F32 = mybir.dt.float32
BF16 = mybir.dt.bfloat16
U32 = mybir.dt.uint32
U8 = mybir.dt.uint8
FP8X4 = mybir.dt.float8_e4m3fn_x4
ADD = mybir.AluOpType.add

P = 128
PACK = 4
BATCH, SEQ, FEATURES = 2, 512, 1024
TOKENS = BATCH * SEQ
BLOCKS = TOKENS // 128
TAPS, HALF = 11, 5
TAP_SLOT = 16
PASSES = FEATURES // (P * PACK)
N_TILE = 512
HALVES = FEATURES // N_TILE
ROW_PAIRS = FEATURES // (2 * P)

WIN_STEP = 112
MARGIN = (P - WIN_STEP) // 2
N_WINDOWS = (TOKENS - P) // WIN_STEP + 1
assert MARGIN >= HALF and (N_WINDOWS - 1) * WIN_STEP + P == TOKENS
SEAM_WINDOW, SEAM = divmod(SEQ, WIN_STEP)
assert (SEAM_WINDOW - 1) * WIN_STEP + P <= SEQ and SEAM == P // 2

ROW_PITCH = 136

ROUND = 2
N_ROUNDS = BLOCKS // ROUND

FLOPS = 2 * 2 * TOKENS * FEATURES * FEATURES + 2 * TOKENS * TAPS * FEATURES


def window_place(w):
    lo = 0 if w == 0 else MARGIN
    hi = P if w == N_WINDOWS - 1 else P - MARGIN
    return w * WIN_STEP, lo, hi


def tile_localattention_pb_kernel(tc, x, Wv, bv, attn_band, Wo, bo, out):
    nc = tc.nc
    x_hbm = x.rearrange("b s d -> (b s) d")
    taps_hbm = attn_band.rearrange("b s o -> (b s) o")
    out_hbm = out.rearrange("b s d -> (b s) d")
    out_flat = out.rearrange("b s d -> (b s d)")
    parked = out_flat[TOKENS * FEATURES - N_WINDOWS * P * ROW_PITCH : TOKENS * FEATURES]

    with ExitStack() as stack:
        keep = stack.enter_context(tc.tile_pool(name="keep", bufs=1))
        x_pool = stack.enter_context(tc.tile_pool(name="x_pool", bufs=BLOCKS))
        sorted_pool = stack.enter_context(tc.tile_pool(name="sorted_pool", bufs=4))
        x_pairs_pool = stack.enter_context(tc.tile_pool(name="x_pairs_pool", bufs=4))
        pairs_pool = stack.enter_context(tc.tile_pool(name="pairs_pool", bufs=3))
        v_pool = stack.enter_context(tc.tile_pool(name="v_pool", bufs=N_WINDOWS))
        out_pool = stack.enter_context(tc.tile_pool(name="out_pool", bufs=4))
        psum = stack.enter_context(tc.psum_pool(name="psum", bufs=4))
        stack.enter_context(tc.manual_schedule())

        ident = keep.tile([P, P], F32)
        make_identity(nc, ident[:])

        bv_row = keep.tile([P, FEATURES], BF16)
        nc.vector.memset(bv_row[:].bitcast(mybir.dt.int32), 0)
        ones = keep.tile([P, P], BF16)
        nc.vector.memset(ones[:], 1.0)

        table_in = keep.tile([P, 1], F32)
        nc.vector.memset(table_in[:], 0.0)
        table_out = keep.tile([P, 1], F32)
        nc.scalar.copy(out=table_out[:], in_=table_in[:])

        x_rows = {}

        def load_x(b):
            x_block = x_pool.tile([P, FEATURES], BF16)
            nc.sync.dma_start(out=x_block[:], in_=x_hbm[b * P : (b + 1) * P, :])
            x_rows[b] = x_block

        load_x(0)
        wv_rows = keep.tile([P, ROW_PAIRS, 2, FEATURES], BF16)
        for q in range(ROW_PAIRS):
            group, upper = divmod(q, 2)
            rows_of_group = Wv[PACK * P * group : PACK * P * (group + 1), :].rearrange(
                "(m t) k -> m t k", t=PACK
            )
            for e in range(2):
                nc.sync.dma_start(
                    out=wv_rows[:, q, e, :], in_=rows_of_group[:, 2 * upper + e, :]
                )
            if q == 0:
                nc.sync.dma_start(out=bv_row[0:1, :], in_=bv.rearrange("(o n) -> o n", o=1))
        taps_win = keep.tile([P, N_WINDOWS, TAP_SLOT], BF16)
        nc.sync.dma_start(
            out=taps_win[0:WIN_STEP, :, 0:TAPS],
            in_=taps_hbm[0 : N_WINDOWS * WIN_STEP, :].rearrange("(w r) o -> r w o", r=WIN_STEP),
        )
        nc.sync.dma_start(
            out=taps_win[WIN_STEP:P, :, 0:TAPS],
            in_=taps_hbm[P - WIN_STEP : TOKENS, :].rearrange("(w r) o -> r w o", r=WIN_STEP)[
                2 * WIN_STEP - P : WIN_STEP
            ],
        )

        padded = keep.tile([P, N_WINDOWS, ROW_PITCH], F32)
        nc.gpsimd.memset(padded[:], 0.0)
        nc.gpsimd.tensor_copy(out=padded[:, :, 0:TAPS], in_=taps_win[:, :, 0:TAPS])
        nc.gpsimd.dma_start(
            out=parked.rearrange("(w p q) -> p w q", p=P, q=ROW_PITCH), in_=padded[:]
        )

        for b in range(1, BLOCKS):
            load_x(b)

        band = keep.tile([P, N_WINDOWS, P], F32)
        nc.sync.dma_start(
            out=band[:],
            in_=parked.rearrange("(w r) -> w r", r=P * ROW_PITCH)[
                :, HALF : HALF + P * (ROW_PITCH - 1)
            ].rearrange("w (p q) -> p w q", q=ROW_PITCH - 1)[:, :, 0:P],
        )
        nc.gpsimd.memset(band[0:SEAM, SEAM_WINDOW, SEAM:P], 0.0)
        nc.gpsimd.memset(band[SEAM:P, SEAM_WINDOW, 0:SEAM], 0.0)

        wo_rows = keep.tile([P, ROW_PAIRS, 2, FEATURES], BF16)
        for q in range(ROW_PAIRS):
            nc.sync.dma_start(
                out=wo_rows[:, q, :, :],
                in_=Wo[2 * P * q : 2 * P * (q + 1), :].rearrange("(j m) k -> m j k", m=P),
            )

        bo_all = keep.tile([P, FEATURES], BF16)
        nc.sync.dma_start(out=bo_all[:], in_=bo.partition_broadcast(P))

        band_t = keep.tile([P, N_WINDOWS, P], F32)

        def transpose_band():
            for w0 in range(0, N_WINDOWS, PACK):
                count = min(PACK, N_WINDOWS - w0)
                flipped = psum.tile([P, PACK, P], F32, tag="flipped")
                for j in range(count):
                    nc.tensor.transpose(flipped[:, j, :], band[:, w0 + j, :], ident[:])
                nc.scalar.copy(out=band_t[:, w0 : w0 + count, :], in_=flipped[:, 0:count, :])

        def sort_words(words, count, copy):
            sorted_words = sorted_pool.tile([P, count, PASSES, 2, P], F32, tag="sorted" + str(count))
            copy(
                out=sorted_words[:].rearrange("p n c u i -> p (n c) u i"),
                in_=words.rearrange("p (n i u) -> p n u i", i=P, u=2),
            )
            return sorted_words

        def unsorted(rows):
            return rows.bitcast(F32).rearrange("p (c i u) -> p c u i", c=PASSES, u=2)

        def transpose_rows(words):
            flipped = psum.tile([P, PACK, P], F32, tag="flipped")
            for c in range(PASSES):
                for u in range(2):
                    nc.tensor.transpose(flipped[:, 2 * c + u, :], words[:, c, u, :], ident[:])
            return flipped[:].rearrange("p (c u) r -> p c r u", u=2)

        x_codes = keep.tile([P, N_WINDOWS, PASSES, P], U32, align_bytes=64)
        x_scales = keep.tile([P, N_WINDOWS, PASSES, P], U8, align_bytes=64)

        x_words = {}

        def sort_x(b):
            x_sorted = sort_words(x_rows[b][:].bitcast(F32), 1, nc.scalar.copy)
            x_words[b] = x_sorted[:, 0, :, :, :]

        x_pairs_of = {}

        def prepare_x(b):
            flipped_pairs = transpose_rows(x_words[b])
            for w in range(N_WINDOWS):
                first = w * WIN_STEP
                start, stop = max(b * P, first), min((b + 1) * P, first + P)
                if start >= stop:
                    continue
                if w not in x_pairs_of:
                    x_pairs = x_pairs_pool.tile([P, PASSES, P, 2], F32, align_bytes=64)
                    x_pairs_of[w] = x_pairs
                nc.scalar.copy(
                    out=x_pairs_of[w][:, :, start - first : stop - first, :],
                    in_=flipped_pairs[:, :, start - b * P : stop - b * P, :],
                )
                if stop == first + P:
                    nc.vector.quantize_mx(
                        out=x_codes[:, w, :, :].rearrange("p c r -> p (c r)").bitcast(FP8X4),
                        scales=x_scales[:, w, :, :].rearrange("p c r -> p (c r)"),
                        in_=x_pairs_of[w][:].rearrange("p c r u -> p (c r u)").bitcast(BF16),
                    )

        def weight_tiles(label):
            codes = keep.tile([P, PASSES, FEATURES], U32, name=label + "_codes", align_bytes=64)
            scales = keep.tile([P, PASSES, FEATURES], U8, name=label + "_scales", align_bytes=64)
            return codes, scales

        def prepare_weight_pair(words, tiles, q, second_copy):
            codes, scales = tiles
            w_pairs = pairs_pool.tile([P, PASSES, 2 * P, 2], F32, align_bytes=64)
            nc.scalar.copy(out=w_pairs[:, :, 0:P, :], in_=transpose_rows(words[0]))
            second_copy(out=w_pairs[:, :, P : 2 * P, :], in_=transpose_rows(words[1]))
            cols = slice(2 * P * q, 2 * P * (q + 1))
            for c in range(PASSES):
                nc.vector.quantize_mx(
                    out=codes[:, c, cols].bitcast(FP8X4),
                    scales=scales[:, c, cols],
                    in_=w_pairs[:, c, :, :].rearrange("p n u -> p (n u)").bitcast(BF16),
                )

        wo_words = {}

        def sort_wo(q):
            wo_sorted = sort_words(
                wo_rows[:, q, :, :].rearrange("p j k -> p (j k)").bitcast(F32), 2, nc.scalar.copy
            )
            wo_words[q] = [wo_sorted[:, j, :, :, :] for j in range(2)]

        wv_tiles = weight_tiles("wv")
        wo_tiles = weight_tiles("wo")

        def product(left_codes, left_scales, tiles):
            codes, scales = tiles
            accs = []
            for half in range(HALVES):
                acc = psum.tile([P, N_TILE], F32, tag="acc")
                accs.append(acc)
            for c in range(PASSES):
                for half in range(HALVES):
                    cols = slice(half * N_TILE, (half + 1) * N_TILE)
                    nc.tensor.matmul_mx(
                        out=accs[half][:],
                        lhsT=left_codes[c].bitcast(FP8X4),
                        lhsT_scale=left_scales[c],
                        rhs=codes[:, c, cols].bitcast(FP8X4),
                        rhs_scale=scales[:, c, cols],
                        start=(c == 0),
                        stop=(c == PASSES - 1),
                    )
            return accs

        bv_all = keep.tile([P, FEATURES], BF16)

        def spread_bv():
            for half in range(HALVES):
                acc = psum.tile([P, N_TILE], F32, tag="acc")
                cols = slice(half * N_TILE, (half + 1) * N_TILE)
                nc.tensor.matmul(
                    out=acc[:], lhsT=ones[:], rhs=bv_row[:, cols], start=True, stop=True
                )
                nc.scalar.copy(
                    out=bv_all[:, cols].rearrange("p (t m) -> p t m", t=PACK),
                    in_=acc[:].rearrange("p (m t) -> p t m", t=PACK),
                )

        v_rows = {}

        def project_v(w):
            v_accs = product(
                [x_codes[:, w, c, :] for c in range(PASSES)],
                [x_scales[:, w, c, :] for c in range(PASSES)],
                wv_tiles,
            )
            v_win = v_pool.tile([P, FEATURES], F32)
            for half in range(HALVES):
                cols = slice(half * N_TILE, (half + 1) * N_TILE)
                nc.vector.tensor_tensor(
                    out=v_win[:, cols], in0=v_accs[half][:], in1=bv_all[:, cols], op=ADD
                )
            v_rows[w] = v_win

        ctx_quads = keep.tile([P, PASSES, TOKENS, PACK], BF16, align_bytes=64)
        ctx_codes = keep.tile([P, PASSES, TOKENS], U32, align_bytes=64)
        ctx_scales = keep.tile([P, PASSES, TOKENS], U8, align_bytes=64)

        def mix(w, c):
            first, lo, hi = window_place(w)
            mixed = psum.tile([P, PACK, P], F32, tag="flipped")
            for t in range(PACK):
                blk = c * PACK + t
                nc.tensor.matmul(
                    out=mixed[:, t, lo:hi],
                    lhsT=v_rows[w][:, blk * P : (blk + 1) * P],
                    rhs=band_t[:, w, lo:hi],
                    start=True,
                    stop=True,
                )
            copy = nc.scalar.copy if (c == 0) == (w < ROW_PAIRS) else nc.vector.tensor_copy
            copy(
                out=ctx_quads[:, c, first + lo : first + hi, :],
                in_=mixed[:, :, lo:hi].rearrange("p t i -> p i t"),
            )

        def quantise_ctx(tb):
            tokens = slice(tb * P, (tb + 1) * P)
            for c in range(PASSES):
                nc.vector.quantize_mx(
                    out=ctx_codes[:, c, tokens].bitcast(FP8X4),
                    scales=ctx_scales[:, c, tokens],
                    in_=ctx_quads[:, c, tokens, :].rearrange("p i t -> p (i t)"),
                )

        def project_out(tb):
            tokens = slice(tb * P, (tb + 1) * P)
            out_accs = product(
                [ctx_codes[:, c, tokens] for c in range(PASSES)],
                [ctx_scales[:, c, tokens] for c in range(PASSES)],
                wo_tiles,
            )
            width = N_TILE // 2 if tb == BLOCKS - 1 else N_TILE
            for start in range(0, FEATURES, width):
                cols = slice(start, start + width)
                half, offset = divmod(start, N_TILE)
                out_sb = out_pool.tile([P, width], F32, tag="out" + str(width))
                nc.vector.tensor_tensor(
                    out=out_sb[:],
                    in0=out_accs[half][:, offset : offset + width],
                    in1=bo_all[:, cols],
                    op=ADD,
                )
                nc.sync.dma_start(out=out_hbm[tokens, cols], in_=out_sb[:])

        for b in range(2 * ROUND):
            x_words[b] = unsorted(x_rows[b][:])
        prepare_x(0)
        for q in range(ROW_PAIRS):
            wv_words = [unsorted(wv_rows[:, q, e, :]) for e in range(2)]
            prepare_weight_pair(wv_words, wv_tiles, q, nc.vector.tensor_copy)
            if q == 0:
                spread_bv()
        for b in range(1, ROUND):
            prepare_x(b)
        wo_sorted = 0
        for r in range(N_ROUNDS):
            for b in range((r + 1) * ROUND, min((r + 2) * ROUND, BLOCKS)):
                prepare_x(b)
            for b in range((r + 2) * ROUND, min((r + 3) * ROUND, BLOCKS)):
                sort_x(b)
            if r == N_ROUNDS - 1:
                transpose_band()
            if r >= N_ROUNDS - 2:
                for q in range(wo_sorted, r - (N_ROUNDS - 2) + 1 + wo_sorted):
                    sort_wo(q)
                wo_sorted += r - (N_ROUNDS - 2) + 1
            for w in range(r * ROUND, (r + 1) * ROUND if r < N_ROUNDS - 1 else N_WINDOWS):
                project_v(w)
        for q in range(wo_sorted, ROW_PAIRS):
            sort_wo(q)

        projected = 0
        for w in range(N_WINDOWS):
            for c in range(PASSES):
                mix(w, c)
            if w < ROW_PAIRS:
                prepare_weight_pair(wo_words[w], wo_tiles, w, nc.scalar.copy)
            if w >= 1:
                quantise_ctx(w - 1)
            if w >= ROW_PAIRS:
                for tb in range(projected, min(w - 1, projected + 2)):
                    project_out(tb)
                projected = min(w - 1, projected + 2)
        project_out(projected)
